import numpy as np
import ml_dtypes

BF16 = ml_dtypes.bfloat16


def bf(x):
    return np.asarray(x, np.float32).astype(BF16)


def f32(x):
    return np.asarray(x, np.float32)


def f64(x):
    return np.asarray(x).astype(np.float64)


def striped(idx):
    return np.tile(idx.reshape(-1, 16).T, (8, 1))


C, D, H, R, S, N = 256, 128, 2, 16, 512, 256


def setup_inputs():
    return {"x": f32(np.random.standard_normal((D, N, R))), "w": bf(np.random.standard_normal((D, C)) / np.sqrt(D)), "base": f32(0.1 * np.random.standard_normal((C, S))), "offs": striped(np.random.permutation(S)[:N])}


def reference(x, w, base, offs):
    idx = offs[:16].T.reshape(-1)
    xbar = f64(x).sum(axis=2) / R
    s = (f64(w).T @ xbar).reshape(H, D, N)
    sq = (s * s).sum(axis=1, keepdims=True)
    val = (s * ((sq / (1.0 + sq)) / np.sqrt(sq))).reshape(C, N)
    res = f64(base).copy()
    res[:, idx] = val
    return res

@@ -1,0 +1,103 @@
+import concourse.mybir as mybir
+from concourse.masks import make_identity
+
+F32 = mybir.dt.float32
+BF16 = mybir.dt.bfloat16
+U16 = mybir.dt.uint16
+MULT = mybir.AluOpType.mult
+ADD = mybir.AluOpType.add
+ACT = mybir.ActivationFunctionType
+
+P = 128
+N = 256
+R = 16
+H = 2
+S = 512
+PIECE = P
+CHUNK = 32
+
+FLOPS = 2 * P * (H * P) * N
+
+
+def tile_capsulelayer_kernel(tc, x, w, base, offs, out):
+    nc = tc.nc
+    with (
+        tc.tile_pool(name="held", bufs=1) as held,
+        tc.tile_pool(name="xin", bufs=N // CHUNK) as xin,
+        tc.tile_pool(name="work", bufs=2) as work,
+        tc.psum_pool(name="psum", bufs=2) as psum,
+    ):
+        offsets = held.tile([P, N // 16], U16, name="offsets")
+        nc.sync.dma_start(offsets[:], offs)
+        w_raw = held.tile([P, H * P], BF16, name="w_raw")
+        nc.scalar.dma_start(w_raw[:], w)
+        queues = (nc.sync, nc.scalar)
+        x_chunks = []
+        for k in range(N // CHUNK):
+            x_chunk = xin.tile([P, CHUNK, R], F32, name="x_chunk")
+            queues[k % 2].dma_start(x_chunk[:], x[:, k * CHUNK : (k + 1) * CHUNK, :])
+            x_chunks.append(x_chunk)
+        windows = []
+        for h in range(H):
+            window = held.tile([P, S], F32, name=f"window{h}")
+            queues[h % 2].dma_start(window[:], base[h * P : (h + 1) * P, :])
+            windows.append(window)
+
+        identity = held.tile([P, P], F32, name="identity")
+        make_identity(nc, identity[:])
+        ones = held.tile([P, P], F32, name="ones")
+        nc.gpsimd.memset(ones[:], 1.0)
+        w_scaled = held.tile([P, H * P], BF16, name="w_scaled")
+        nc.scalar.mul(w_scaled[:], w_raw[:], 1.0 / R)
+
+        x_sum = held.tile([P, N], BF16, name="x_sum")
+
+        for p in range(N // PIECE):
+            samples = slice(p * PIECE, (p + 1) * PIECE)
+
+            with nc.allow_low_precision(reason="xbar is rounded once to bfloat16 by the statement"):
+                for k in range(p * PIECE // CHUNK, (p + 1) * PIECE // CHUNK):
+                    nc.vector.tensor_reduce(
+                        x_sum[:, k * CHUNK : (k + 1) * CHUNK], x_chunks[k][:], mybir.AxisListType.X, ADD
+                    )
+
+            s_by_sample = psum.tile([P, H * P], F32, name="s_by_sample")
+            nc.tensor.matmul(s_by_sample[:], x_sum[:, samples], w_scaled[:])
+            s_psum = psum.tile([P, H, PIECE], F32, name="s_psum")
+            for h in range(H):
+                nc.tensor.matmul(s_psum[:, h, :], w_scaled[:, h * P : (h + 1) * P], x_sum[:, samples])
+
+            sq = work.tile([P, H], F32, name="sq")
+            for h in range(H):
+                squares = work.tile([P, P], BF16, name="squares")
+                nc.scalar.activation(
+                    squares[:], s_by_sample[:, h * P : (h + 1) * P], ACT.Square, accum_out=sq[:, h : h + 1]
+                )
+            root = work.tile([P, H], F32, name="root")
+            nc.scalar.activation(root[:], sq[:], ACT.Sqrt)
+            recip = work.tile([P, H], F32, name="recip")
+            nc.vector.tensor_scalar(recip[:], sq[:], 1.0, None, ADD)
+            nc.vector.reciprocal(recip[:], recip[:])
+
+            s_sbuf = work.tile([P, H, PIECE], F32, name="s_sbuf")
+            nc.scalar.copy(s_sbuf[:], s_psum[:])
+
+            diagonal = work.tile([P, H, PIECE], F32, name="diagonal")
+            scale_psum = psum.tile([P, H, PIECE], F32, name="scale_psum")
+            for h in range(H):
+                nc.vector.tensor_scalar(
+                    diagonal[:, h, :], identity[:], root[:, h : h + 1], recip[:, h : h + 1], MULT, MULT
+                )
+                nc.tensor.matmul(scale_psum[:, h, :], ones[:], diagonal[:, h, :])
+            scale = work.tile([P, H, PIECE], F32, name="scale")
+            for h in range(H):
+                nc.scalar.copy(scale[:, h, :], scale_psum[:, h, :])
+
+            piece_offsets = offsets[:, p * (PIECE // 16) : (p + 1) * (PIECE // 16)]
+            for h in range(H):
+                nc.vector.tensor_tensor(
+                    windows[h][:].indirect(piece_offsets), s_sbuf[:, h, :], scale[:, h, :], MULT
+                )
+
+        for h in range(H):
+            queues[h % 2].dma_start(out[h * P : (h + 1) * P, :], windows[h][:])

@@ -31,73 +31,87 @@ def tile_capsulelayer_kernel(tc, x, w, base, offs, out):
         nc.sync.dma_start(offsets[:], offs)
         w_raw = held.tile([P, H * P], BF16, name="w_raw")
         nc.scalar.dma_start(w_raw[:], w)
-        queues = (nc.sync, nc.scalar)
         x_chunks = []
         for k in range(N // CHUNK):
             x_chunk = xin.tile([P, CHUNK, R], F32, name="x_chunk")
-            queues[k % 2].dma_start(x_chunk[:], x[:, k * CHUNK : (k + 1) * CHUNK, :])
+            nc.sync.dma_start(x_chunk[:], x[:, k * CHUNK : (k + 1) * CHUNK, :])
             x_chunks.append(x_chunk)
         windows = []
         for h in range(H):
             window = held.tile([P, S], F32, name=f"window{h}")
-            queues[h % 2].dma_start(window[:], base[h * P : (h + 1) * P, :])
+            nc.sync.dma_start(window[:], base[h * P : (h + 1) * P, :])
             windows.append(window)
 
         identity = held.tile([P, P], F32, name="identity")
         make_identity(nc, identity[:])
         ones = held.tile([P, P], F32, name="ones")
         nc.gpsimd.memset(ones[:], 1.0)
+        warm = held.tile([P, 1], F32, name="warm")
+        nc.scalar.activation(warm[:], ones[:, 0:1], ACT.Sqrt)
         w_scaled = held.tile([P, H * P], BF16, name="w_scaled")
         nc.scalar.mul(w_scaled[:], w_raw[:], 1.0 / R)
 
         x_sum = held.tile([P, N], BF16, name="x_sum")
 
-        for p in range(N // PIECE):
-            samples = slice(p * PIECE, (p + 1) * PIECE)
-
+        def add_route_nodes(k):
             with nc.allow_low_precision(reason="xbar is rounded once to bfloat16 by the statement"):
-                for k in range(p * PIECE // CHUNK, (p + 1) * PIECE // CHUNK):
-                    nc.vector.tensor_reduce(
-                        x_sum[:, k * CHUNK : (k + 1) * CHUNK], x_chunks[k][:], mybir.AxisListType.X, ADD
-                    )
+                nc.vector.tensor_reduce(
+                    x_sum[:, k * CHUNK : (k + 1) * CHUNK], x_chunks[k][:], mybir.AxisListType.X, ADD
+                )
 
+        def project(p):
+            samples = slice(p * PIECE, (p + 1) * PIECE)
             s_by_sample = psum.tile([P, H * P], F32, name="s_by_sample")
             nc.tensor.matmul(s_by_sample[:], x_sum[:, samples], w_scaled[:])
             s_psum = psum.tile([P, H, PIECE], F32, name="s_psum")
             for h in range(H):
                 nc.tensor.matmul(s_psum[:, h, :], w_scaled[:, h * P : (h + 1) * P], x_sum[:, samples])
-
             sq = work.tile([P, H], F32, name="sq")
             for h in range(H):
                 squares = work.tile([P, P], BF16, name="squares")
                 nc.scalar.activation(
                     squares[:], s_by_sample[:, h * P : (h + 1) * P], ACT.Square, accum_out=sq[:, h : h + 1]
                 )
+            return s_psum, sq
+
+        def squash_factor(s_psum, sq):
             root = work.tile([P, H], F32, name="root")
             nc.scalar.activation(root[:], sq[:], ACT.Sqrt)
             recip = work.tile([P, H], F32, name="recip")
             nc.vector.tensor_scalar(recip[:], sq[:], 1.0, None, ADD)
             nc.vector.reciprocal(recip[:], recip[:])
-
-            s_sbuf = work.tile([P, H, PIECE], F32, name="s_sbuf")
-            nc.scalar.copy(s_sbuf[:], s_psum[:])
-
-            diagonal = work.tile([P, H, PIECE], F32, name="diagonal")
+            rows = work.tile([P, H, P], F32, name="rows")
             scale_psum = psum.tile([P, H, PIECE], F32, name="scale_psum")
-            for h in range(H):
-                nc.vector.tensor_scalar(
-                    diagonal[:, h, :], identity[:], root[:, h : h + 1], recip[:, h : h + 1], MULT, MULT
-                )
-                nc.tensor.matmul(scale_psum[:, h, :], ones[:], diagonal[:, h, :])
             scale = work.tile([P, H, PIECE], F32, name="scale")
             for h in range(H):
+                nc.vector.tensor_scalar(
+                    rows[:, h, :], ones[:], root[:, h : h + 1], recip[:, h : h + 1], MULT, MULT
+                )
+                nc.tensor.transpose(scale_psum[:, h, :], rows[:, h, :], identity[:])
                 nc.scalar.copy(scale[:, h, :], scale_psum[:, h, :])
+            s_sbuf = work.tile([P, H, PIECE], F32, name="s_sbuf")
+            nc.scalar.copy(s_sbuf[:], s_psum[:])
+            return s_sbuf, scale
 
+        def place(p, s_sbuf, scale):
             piece_offsets = offsets[:, p * (PIECE // 16) : (p + 1) * (PIECE // 16)]
             for h in range(H):
                 nc.vector.tensor_tensor(
                     windows[h][:].indirect(piece_offsets), s_sbuf[:, h, :], scale[:, h, :], MULT
                 )
 
+        for k in range(0, 4):
+            add_route_nodes(k)
+        first = project(0)
+        for k in range(4, 6):
+            add_route_nodes(k)
+        first = squash_factor(*first)
+        for k in range(6, 8):
+            add_route_nodes(k)
+        second = squash_factor(*project(1))
+        place(0, *first)
+        place(1, *second)
+
+        stores = (nc.sync, nc.scalar)
         for h in range(H):
-            queues[h % 2].dma_start(out[h * P : (h + 1) * P, :], windows[h][:])
+            stores[h].dma_start(out[h * P : (h + 1) * P, :], windows[h][:])

@@ -14,7 +14,8 @@ R = 16
 H = 2
 S = 512
 PIECE = P
-CHUNK = 32
+CHUNKS = (32, 32, 32, 32, 32, 32, 32, 16, 8, 8)
+assert sum(CHUNKS) == N and sum(CHUNKS[:4]) == PIECE
 
 FLOPS = 2 * P * (H * P) * N
 
@@ -23,19 +24,20 @@ def tile_capsulelayer_kernel(tc, x, w, base, offs, out):
     nc = tc.nc
     with (
         tc.tile_pool(name="held", bufs=1) as held,
-        tc.tile_pool(name="xin", bufs=N // CHUNK) as xin,
+        tc.tile_pool(name="xin", bufs=len(CHUNKS)) as xin,
         tc.tile_pool(name="work", bufs=2) as work,
         tc.psum_pool(name="psum", bufs=2) as psum,
     ):
-        offsets = held.tile([P, N // 16], U16, name="offsets")
-        nc.sync.dma_start(offsets[:], offs)
         w_raw = held.tile([P, H * P], BF16, name="w_raw")
         nc.scalar.dma_start(w_raw[:], w)
         x_chunks = []
-        for k in range(N // CHUNK):
-            x_chunk = xin.tile([P, CHUNK, R], F32, name="x_chunk")
-            nc.sync.dma_start(x_chunk[:], x[:, k * CHUNK : (k + 1) * CHUNK, :])
+        for k, size in enumerate(CHUNKS):
+            start = sum(CHUNKS[:k])
+            x_chunk = xin.tile([P, max(CHUNKS), R], F32, name="x_chunk")
+            nc.sync.dma_start(x_chunk[:, :size, :], x[:, start : start + size, :])
             x_chunks.append(x_chunk)
+        offsets = held.tile([P, N // 16], U16, name="offsets")
+        nc.sync.dma_start(offsets[:], offs)
         windows = []
         for h in range(H):
             window = held.tile([P, S], F32, name=f"window{h}")
@@ -44,10 +46,9 @@ def tile_capsulelayer_kernel(tc, x, w, base, offs, out):
 
         identity = held.tile([P, P], F32, name="identity")
         make_identity(nc, identity[:])
-        ones = held.tile([P, P], F32, name="ones")
-        nc.gpsimd.memset(ones[:], 1.0)
         warm = held.tile([P, 1], F32, name="warm")
-        nc.scalar.activation(warm[:], ones[:, 0:1], ACT.Sqrt)
+        nc.gpsimd.memset(warm[:], 1.0)
+        nc.scalar.activation(warm[:], warm[:], ACT.Sqrt)
         w_scaled = held.tile([P, H * P], BF16, name="w_scaled")
         nc.scalar.mul(w_scaled[:], w_raw[:], 1.0 / R)
 
@@ -55,63 +56,70 @@ def tile_capsulelayer_kernel(tc, x, w, base, offs, out):
 
         def add_route_nodes(k):
             with nc.allow_low_precision(reason="xbar is rounded once to bfloat16 by the statement"):
+                start = sum(CHUNKS[:k])
                 nc.vector.tensor_reduce(
-                    x_sum[:, k * CHUNK : (k + 1) * CHUNK], x_chunks[k][:], mybir.AxisListType.X, ADD
+                    x_sum[:, start : start + CHUNKS[k]],
+                    x_chunks[k][:, : CHUNKS[k], :],
+                    mybir.AxisListType.X,
+                    ADD,
                 )
 
-        def project(p):
-            samples = slice(p * PIECE, (p + 1) * PIECE)
+        def squared_norms(p):
             s_by_sample = psum.tile([P, H * P], F32, name="s_by_sample")
-            nc.tensor.matmul(s_by_sample[:], x_sum[:, samples], w_scaled[:])
-            s_psum = psum.tile([P, H, PIECE], F32, name="s_psum")
-            for h in range(H):
-                nc.tensor.matmul(s_psum[:, h, :], w_scaled[:, h * P : (h + 1) * P], x_sum[:, samples])
+            nc.tensor.matmul(s_by_sample[:], x_sum[:, p * PIECE : (p + 1) * PIECE], w_scaled[:])
             sq = work.tile([P, H], F32, name="sq")
             for h in range(H):
                 squares = work.tile([P, P], BF16, name="squares")
                 nc.scalar.activation(
                     squares[:], s_by_sample[:, h * P : (h + 1) * P], ACT.Square, accum_out=sq[:, h : h + 1]
                 )
-            return s_psum, sq
+            return sq
 
-        def squash_factor(s_psum, sq):
-            root = work.tile([P, H], F32, name="root")
-            nc.scalar.activation(root[:], sq[:], ACT.Sqrt)
+        def squash_factor_squared(sq):
             recip = work.tile([P, H], F32, name="recip")
             nc.vector.tensor_scalar(recip[:], sq[:], 1.0, None, ADD)
             nc.vector.reciprocal(recip[:], recip[:])
             rows = work.tile([P, H, P], F32, name="rows")
-            scale_psum = psum.tile([P, H, PIECE], F32, name="scale_psum")
-            scale = work.tile([P, H, PIECE], F32, name="scale")
+            scale2_psum = psum.tile([P, H, PIECE], F32, name="scale2_psum")
             for h in range(H):
                 nc.vector.tensor_scalar(
-                    rows[:, h, :], ones[:], root[:, h : h + 1], recip[:, h : h + 1], MULT, MULT
+                    rows[:, h, :],
+                    sq[:, h : h + 1].to_broadcast([P, P]),
+                    recip[:, h : h + 1],
+                    recip[:, h : h + 1],
+                    MULT,
+                    MULT,
                 )
-                nc.tensor.transpose(scale_psum[:, h, :], rows[:, h, :], identity[:])
-                nc.scalar.copy(scale[:, h, :], scale_psum[:, h, :])
+                nc.tensor.transpose(scale2_psum[:, h, :], rows[:, h, :], identity[:])
+            return scale2_psum
+
+        def place(p, scale2_psum):
+            s_psum = psum.tile([P, H, PIECE], F32, name="s_psum")
+            for h in range(H):
+                nc.tensor.matmul(
+                    s_psum[:, h, :], w_scaled[:, h * P : (h + 1) * P], x_sum[:, p * PIECE : (p + 1) * PIECE]
+                )
             s_sbuf = work.tile([P, H, PIECE], F32, name="s_sbuf")
             nc.scalar.copy(s_sbuf[:], s_psum[:])
-            return s_sbuf, scale
-
-        def place(p, s_sbuf, scale):
+            scale = work.tile([P, H, PIECE], F32, name="scale")
             piece_offsets = offsets[:, p * (PIECE // 16) : (p + 1) * (PIECE // 16)]
             for h in range(H):
+                nc.scalar.activation(scale[:, h, :], scale2_psum[:, h, :], ACT.Sqrt)
                 nc.vector.tensor_tensor(
                     windows[h][:].indirect(piece_offsets), s_sbuf[:, h, :], scale[:, h, :], MULT
                 )
 
         for k in range(0, 4):
             add_route_nodes(k)
-        first = project(0)
+        sq_first = squared_norms(0)
         for k in range(4, 6):
             add_route_nodes(k)
-        first = squash_factor(*first)
-        for k in range(6, 8):
+        scale2_first = squash_factor_squared(sq_first)
+        for k in range(6, len(CHUNKS)):
             add_route_nodes(k)
-        second = squash_factor(*project(1))
-        place(0, *first)
-        place(1, *second)
+        scale2_second = squash_factor_squared(squared_norms(1))
+        place(0, scale2_first)
+        place(1, scale2_second)
 
-        stores = (nc.sync, nc.scalar)
         for h in range(H):
-            stores[h].dma_start(out[h * P : (h + 1) * P, :], windows[h][:])
+            nc.sync.dma_start(out[h * P : (h + 1) * P, :], windows[h][:])

@@ -14,8 +14,8 @@ R = 16
 H = 2
 S = 512
 PIECE = P
-CHUNKS = (32, 32, 32, 32, 32, 32, 32, 16, 8, 8)
-assert sum(CHUNKS) == N and sum(CHUNKS[:4]) == PIECE
+CHUNKS = (64, 64, 64, 32, 16, 16)
+assert sum(CHUNKS) == N and sum(CHUNKS[:2]) == PIECE
 
 FLOPS = 2 * P * (H * P) * N
 
@@ -26,7 +26,8 @@ def tile_capsulelayer_kernel(tc, x, w, base, offs, out):
         tc.tile_pool(name="held", bufs=1) as held,
         tc.tile_pool(name="xin", bufs=len(CHUNKS)) as xin,
         tc.tile_pool(name="work", bufs=2) as work,
-        tc.psum_pool(name="psum", bufs=2) as psum,
+        tc.psum_pool(name="psum", bufs=1) as psum,
+        tc.psum_pool(name="psum_factor", bufs=2) as psum_factor,
     ):
         w_raw = held.tile([P, H * P], BF16, name="w_raw")
         nc.scalar.dma_start(w_raw[:], w)
@@ -65,23 +66,23 @@ def tile_capsulelayer_kernel(tc, x, w, base, offs, out):
                 )
 
         def squared_norms(p):
-            s_by_sample = psum.tile([P, H * P], F32, name="s_by_sample")
-            nc.tensor.matmul(s_by_sample[:], x_sum[:, p * PIECE : (p + 1) * PIECE], w_scaled[:])
             sq = work.tile([P, H], F32, name="sq")
             for h in range(H):
-                squares = work.tile([P, P], BF16, name="squares")
-                nc.scalar.activation(
-                    squares[:], s_by_sample[:, h * P : (h + 1) * P], ACT.Square, accum_out=sq[:, h : h + 1]
+                s_by_sample = psum.tile([P, P], F32, name=f"s_by_sample{h}")
+                nc.tensor.matmul(
+                    s_by_sample[:], x_sum[:, p * PIECE : (p + 1) * PIECE], w_scaled[:, h * P : (h + 1) * P]
                 )
+                squares = work.tile([P, P], BF16, name="squares")
+                nc.scalar.activation(squares[:], s_by_sample[:], ACT.Square, accum_out=sq[:, h : h + 1])
             return sq
 
         def squash_factor_squared(sq):
             recip = work.tile([P, H], F32, name="recip")
-            nc.vector.tensor_scalar(recip[:], sq[:], 1.0, None, ADD)
-            nc.vector.reciprocal(recip[:], recip[:])
             rows = work.tile([P, H, P], F32, name="rows")
-            scale2_psum = psum.tile([P, H, PIECE], F32, name="scale2_psum")
+            scale2_psum = []
             for h in range(H):
+                nc.vector.tensor_scalar(recip[:, h : h + 1], sq[:, h : h + 1], 1.0, None, ADD)
+                nc.vector.reciprocal(recip[:, h : h + 1], recip[:, h : h + 1])
                 nc.vector.tensor_scalar(
                     rows[:, h, :],
                     sq[:, h : h + 1].to_broadcast([P, P]),
@@ -90,7 +91,8 @@ def tile_capsulelayer_kernel(tc, x, w, base, offs, out):
                     MULT,
                     MULT,
                 )
-                nc.tensor.transpose(scale2_psum[:, h, :], rows[:, h, :], identity[:])
+                scale2_psum.append(psum_factor.tile([P, PIECE], F32, name=f"scale2_psum{h}"))
+                nc.tensor.transpose(scale2_psum[h][:], rows[:, h, :], identity[:])
             return scale2_psum
 
         def place(p, scale2_psum):
@@ -104,18 +106,17 @@ def tile_capsulelayer_kernel(tc, x, w, base, offs, out):
             scale = work.tile([P, H, PIECE], F32, name="scale")
             piece_offsets = offsets[:, p * (PIECE // 16) : (p + 1) * (PIECE // 16)]
             for h in range(H):
-                nc.scalar.activation(scale[:, h, :], scale2_psum[:, h, :], ACT.Sqrt)
+                nc.scalar.activation(scale[:, h, :], scale2_psum[h][:], ACT.Sqrt)
                 nc.vector.tensor_tensor(
                     windows[h][:].indirect(piece_offsets), s_sbuf[:, h, :], scale[:, h, :], MULT
                 )
 
-        for k in range(0, 4):
+        for k in range(0, 2):
             add_route_nodes(k)
         sq_first = squared_norms(0)
-        for k in range(4, 6):
-            add_route_nodes(k)
+        add_route_nodes(2)
         scale2_first = squash_factor_squared(sq_first)
-        for k in range(6, len(CHUNKS)):
+        for k in range(3, len(CHUNKS)):
             add_route_nodes(k)
         scale2_second = squash_factor_squared(squared_norms(1))
         place(0, scale2_first)

@@ -14,8 +14,8 @@ R = 16
 H = 2
 S = 512
 PIECE = P
-CHUNKS = (64, 64, 64, 32, 16, 16)
-assert sum(CHUNKS) == N and sum(CHUNKS[:2]) == PIECE
+CHUNKS = (32, 32, 64, 64, 32, 16, 16)
+assert sum(CHUNKS) == N and sum(CHUNKS[:3]) == PIECE
 
 FLOPS = 2 * P * (H * P) * N
 
@@ -111,12 +111,12 @@ def tile_capsulelayer_kernel(tc, x, w, base, offs, out):
                     windows[h][:].indirect(piece_offsets), s_sbuf[:, h, :], scale[:, h, :], MULT
                 )
 
-        for k in range(0, 2):
+        for k in range(0, 3):
             add_route_nodes(k)
         sq_first = squared_norms(0)
-        add_route_nodes(2)
+        add_route_nodes(3)
         scale2_first = squash_factor_squared(sq_first)
-        for k in range(3, len(CHUNKS)):
+        for k in range(4, len(CHUNKS)):
             add_route_nodes(k)
         scale2_second = squash_factor_squared(squared_norms(1))
         place(0, scale2_first)

@@ -78,21 +78,16 @@ def tile_capsulelayer_kernel(tc, x, w, base, offs, out):
 
         def squash_factor_squared(sq):
             recip = work.tile([P, H], F32, name="recip")
-            rows = work.tile([P, H, P], F32, name="rows")
+            scale2 = work.tile([P, H], F32, name="scale2")
             scale2_psum = []
             for h in range(H):
                 nc.vector.tensor_scalar(recip[:, h : h + 1], sq[:, h : h + 1], 1.0, None, ADD)
                 nc.vector.reciprocal(recip[:, h : h + 1], recip[:, h : h + 1])
                 nc.vector.tensor_scalar(
-                    rows[:, h, :],
-                    sq[:, h : h + 1].to_broadcast([P, P]),
-                    recip[:, h : h + 1],
-                    recip[:, h : h + 1],
-                    MULT,
-                    MULT,
+                    scale2[:, h : h + 1], sq[:, h : h + 1], recip[:, h : h + 1], recip[:, h : h + 1], MULT, MULT
                 )
                 scale2_psum.append(psum_factor.tile([P, PIECE], F32, name=f"scale2_psum{h}"))
-                nc.tensor.transpose(scale2_psum[h][:], rows[:, h, :], identity[:])
+                nc.tensor.transpose(scale2_psum[h][:], scale2[:, h : h + 1].to_broadcast([P, P]), identity[:])
             return scale2_psum
 
         def place(p, scale2_psum):

@@ -14,8 +14,11 @@ R = 16
 H = 2
 S = 512
 PIECE = P
+PIECES = N // PIECE
+LIST_COLUMNS = PIECE // 16
+
 CHUNKS = (32, 32, 64, 64, 32, 16, 16)
-assert sum(CHUNKS) == N and sum(CHUNKS[:3]) == PIECE
+assert sum(CHUNKS) == N
 
 FLOPS = 2 * P * (H * P) * N
 
@@ -25,9 +28,9 @@ def tile_capsulelayer_kernel(tc, x, w, base, offs, out):
     with (
         tc.tile_pool(name="held", bufs=1) as held,
         tc.tile_pool(name="xin", bufs=len(CHUNKS)) as xin,
-        tc.tile_pool(name="work", bufs=2) as work,
+        tc.tile_pool(name="work", bufs=PIECES) as work,
         tc.psum_pool(name="psum", bufs=1) as psum,
-        tc.psum_pool(name="psum_factor", bufs=2) as psum_factor,
+        tc.psum_pool(name="psum_factor", bufs=PIECES) as psum_factor,
     ):
         w_raw = held.tile([P, H * P], BF16, name="w_raw")
         nc.scalar.dma_start(w_raw[:], w)
@@ -54,68 +57,48 @@ def tile_capsulelayer_kernel(tc, x, w, base, offs, out):
         nc.scalar.mul(w_scaled[:], w_raw[:], 1.0 / R)
 
         x_sum = held.tile([P, N], BF16, name="x_sum")
-
-        def add_route_nodes(k):
-            with nc.allow_low_precision(reason="xbar is rounded once to bfloat16 by the statement"):
+        with nc.allow_low_precision(reason="the statement rounds xbar to bfloat16"):
+            for k, size in enumerate(CHUNKS):
                 start = sum(CHUNKS[:k])
                 nc.vector.tensor_reduce(
-                    x_sum[:, start : start + CHUNKS[k]],
-                    x_chunks[k][:, : CHUNKS[k], :],
-                    mybir.AxisListType.X,
-                    ADD,
+                    x_sum[:, start : start + size], x_chunks[k][:, :size, :], mybir.AxisListType.X, ADD
                 )
 
-        def squared_norms(p):
+        scale2_psum = {}
+        for p in range(PIECES):
+            samples = slice(p * PIECE, (p + 1) * PIECE)
             sq = work.tile([P, H], F32, name="sq")
-            for h in range(H):
-                s_by_sample = psum.tile([P, P], F32, name=f"s_by_sample{h}")
-                nc.tensor.matmul(
-                    s_by_sample[:], x_sum[:, p * PIECE : (p + 1) * PIECE], w_scaled[:, h * P : (h + 1) * P]
-                )
-                squares = work.tile([P, P], BF16, name="squares")
-                nc.scalar.activation(squares[:], s_by_sample[:], ACT.Square, accum_out=sq[:, h : h + 1])
-            return sq
-
-        def squash_factor_squared(sq):
             recip = work.tile([P, H], F32, name="recip")
             scale2 = work.tile([P, H], F32, name="scale2")
-            scale2_psum = []
             for h in range(H):
-                nc.vector.tensor_scalar(recip[:, h : h + 1], sq[:, h : h + 1], 1.0, None, ADD)
-                nc.vector.reciprocal(recip[:, h : h + 1], recip[:, h : h + 1])
+                capsule = slice(h * P, (h + 1) * P)
+                column = slice(h, h + 1)
+                s_by_sample = psum.tile([P, P], F32, name=f"s_by_sample{h}")
+                nc.tensor.matmul(s_by_sample[:], x_sum[:, samples], w_scaled[:, capsule])
+                squares = work.tile([P, P], BF16, name="squares")
+                nc.scalar.activation(squares[:], s_by_sample[:], ACT.Square, accum_out=sq[:, column])
+                nc.vector.tensor_scalar(recip[:, column], sq[:, column], 1.0, None, ADD)
+                nc.vector.reciprocal(recip[:, column], recip[:, column])
                 nc.vector.tensor_scalar(
-                    scale2[:, h : h + 1], sq[:, h : h + 1], recip[:, h : h + 1], recip[:, h : h + 1], MULT, MULT
+                    scale2[:, column], sq[:, column], recip[:, column], recip[:, column], MULT, MULT
                 )
-                scale2_psum.append(psum_factor.tile([P, PIECE], F32, name=f"scale2_psum{h}"))
-                nc.tensor.transpose(scale2_psum[h][:], scale2[:, h : h + 1].to_broadcast([P, P]), identity[:])
-            return scale2_psum
+                scale2_psum[p, h] = psum_factor.tile([P, PIECE], F32, name=f"scale2_psum{h}")
+                nc.tensor.transpose(scale2_psum[p, h][:], scale2[:, column].to_broadcast([P, P]), identity[:])
 
-        def place(p, scale2_psum):
+        for p in range(PIECES):
+            samples = slice(p * PIECE, (p + 1) * PIECE)
             s_psum = psum.tile([P, H, PIECE], F32, name="s_psum")
             for h in range(H):
-                nc.tensor.matmul(
-                    s_psum[:, h, :], w_scaled[:, h * P : (h + 1) * P], x_sum[:, p * PIECE : (p + 1) * PIECE]
-                )
+                nc.tensor.matmul(s_psum[:, h, :], w_scaled[:, h * P : (h + 1) * P], x_sum[:, samples])
             s_sbuf = work.tile([P, H, PIECE], F32, name="s_sbuf")
             nc.scalar.copy(s_sbuf[:], s_psum[:])
             scale = work.tile([P, H, PIECE], F32, name="scale")
-            piece_offsets = offsets[:, p * (PIECE // 16) : (p + 1) * (PIECE // 16)]
+            piece_offsets = offsets[:, p * LIST_COLUMNS : (p + 1) * LIST_COLUMNS]
             for h in range(H):
-                nc.scalar.activation(scale[:, h, :], scale2_psum[h][:], ACT.Sqrt)
+                nc.scalar.activation(scale[:, h, :], scale2_psum[p, h][:], ACT.Sqrt)
                 nc.vector.tensor_tensor(
                     windows[h][:].indirect(piece_offsets), s_sbuf[:, h, :], scale[:, h, :], MULT
                 )
-
-        for k in range(0, 3):
-            add_route_nodes(k)
-        sq_first = squared_norms(0)
-        add_route_nodes(3)
-        scale2_first = squash_factor_squared(sq_first)
-        for k in range(4, len(CHUNKS)):
-            add_route_nodes(k)
-        scale2_second = squash_factor_squared(squared_norms(1))
-        place(0, scale2_first)
-        place(1, scale2_second)
 
         for h in range(H):
             nc.sync.dma_start(out[h * P : (h + 1) * P, :], windows[h][:])

@@ -17,7 +17,7 @@ PIECE = P
 PIECES = N // PIECE
 LIST_COLUMNS = PIECE // 16
 
-CHUNKS = (32, 32, 64, 64, 32, 16, 16)
+CHUNKS = (32, 32, 32, 32, 32, 32, 32, 16, 16)
 assert sum(CHUNKS) == N
 
 FLOPS = 2 * P * (H * P) * N
@@ -64,8 +64,8 @@ def tile_capsulelayer_kernel(tc, x, w, base, offs, out):
                     x_sum[:, start : start + size], x_chunks[k][:, :size, :], mybir.AxisListType.X, ADD
                 )
 
-        scale2_psum = {}
         for p in range(PIECES):
+            scale2_psum = []
             samples = slice(p * PIECE, (p + 1) * PIECE)
             sq = work.tile([P, H], F32, name="sq")
             recip = work.tile([P, H], F32, name="recip")
@@ -82,11 +82,9 @@ def tile_capsulelayer_kernel(tc, x, w, base, offs, out):
                 nc.vector.tensor_scalar(
                     scale2[:, column], sq[:, column], recip[:, column], recip[:, column], MULT, MULT
                 )
-                scale2_psum[p, h] = psum_factor.tile([P, PIECE], F32, name=f"scale2_psum{h}")
-                nc.tensor.transpose(scale2_psum[p, h][:], scale2[:, column].to_broadcast([P, P]), identity[:])
+                scale2_psum.append(psum_factor.tile([P, PIECE], F32, name=f"scale2_psum{h}"))
+                nc.tensor.transpose(scale2_psum[h][:], scale2[:, column].to_broadcast([P, P]), identity[:])
 
-        for p in range(PIECES):
-            samples = slice(p * PIECE, (p + 1) * PIECE)
             s_psum = psum.tile([P, H, PIECE], F32, name="s_psum")
             for h in range(H):
                 nc.tensor.matmul(s_psum[:, h, :], w_scaled[:, h * P : (h + 1) * P], x_sum[:, samples])
@@ -95,7 +93,7 @@ def tile_capsulelayer_kernel(tc, x, w, base, offs, out):
             scale = work.tile([P, H, PIECE], F32, name="scale")
             piece_offsets = offsets[:, p * LIST_COLUMNS : (p + 1) * LIST_COLUMNS]
             for h in range(H):
-                nc.scalar.activation(scale[:, h, :], scale2_psum[p, h][:], ACT.Sqrt)
+                nc.scalar.activation(scale[:, h, :], scale2_psum[h][:], ACT.Sqrt)
                 nc.vector.tensor_tensor(
                     windows[h][:].indirect(piece_offsets), s_sbuf[:, h, :], scale[:, h, :], MULT
                 )

@@ -52,7 +52,7 @@ def tile_capsulelayer_kernel(tc, x, w, base, offs, out):
         make_identity(nc, identity[:])
         warm = held.tile([P, 1], F32, name="warm")
         nc.gpsimd.memset(warm[:], 1.0)
-        nc.scalar.activation(warm[:], warm[:], ACT.Sqrt)
+        nc.scalar.activation(warm[:], warm[:], ACT.Abs_reciprocal_sqrt)
         w_scaled = held.tile([P, H * P], BF16, name="w_scaled")
         nc.scalar.mul(w_scaled[:], w_raw[:], 1.0 / R)
 
@@ -65,25 +65,27 @@ def tile_capsulelayer_kernel(tc, x, w, base, offs, out):
                 )
 
         for p in range(PIECES):
-            scale2_psum = []
             samples = slice(p * PIECE, (p + 1) * PIECE)
             sq = work.tile([P, H], F32, name="sq")
-            recip = work.tile([P, H], F32, name="recip")
-            scale2 = work.tile([P, H], F32, name="scale2")
             for h in range(H):
-                capsule = slice(h * P, (h + 1) * P)
-                column = slice(h, h + 1)
                 s_by_sample = psum.tile([P, P], F32, name=f"s_by_sample{h}")
-                nc.tensor.matmul(s_by_sample[:], x_sum[:, samples], w_scaled[:, capsule])
+                nc.tensor.matmul(s_by_sample[:], x_sum[:, samples], w_scaled[:, h * P : (h + 1) * P])
                 squares = work.tile([P, P], BF16, name="squares")
-                nc.scalar.activation(squares[:], s_by_sample[:], ACT.Square, accum_out=sq[:, column])
-                nc.vector.tensor_scalar(recip[:, column], sq[:, column], 1.0, None, ADD)
-                nc.vector.reciprocal(recip[:, column], recip[:, column])
-                nc.vector.tensor_scalar(
-                    scale2[:, column], sq[:, column], recip[:, column], recip[:, column], MULT, MULT
+                nc.scalar.activation(squares[:], s_by_sample[:], ACT.Square, accum_out=sq[:, h : h + 1])
+            rsqrt_sq = work.tile([P, H], F32, name="rsqrt_sq")
+            nc.scalar.activation(rsqrt_sq[:], sq[:], ACT.Abs_reciprocal_sqrt)
+            inverse2 = work.tile([P, H], F32, name="inverse2")
+            inverse2_psum = []
+            for h in range(H):
+                column = slice(h, h + 1)
+                nc.scalar.activation(
+                    inverse2[:, column], sq[:, column], ACT.Square,
+                    bias=rsqrt_sq[:, column], scale=rsqrt_sq[:, column],
                 )
-                scale2_psum.append(psum_factor.tile([P, PIECE], F32, name=f"scale2_psum{h}"))
-                nc.tensor.transpose(scale2_psum[h][:], scale2[:, column].to_broadcast([P, P]), identity[:])
+                inverse2_psum.append(psum_factor.tile([P, PIECE], F32, name=f"inverse2_psum{h}"))
+                nc.tensor.transpose(
+                    inverse2_psum[h][:], inverse2[:, column].to_broadcast([P, P]), identity[:]
+                )
 
             s_psum = psum.tile([P, H, PIECE], F32, name="s_psum")
             for h in range(H):
@@ -93,7 +95,7 @@ def tile_capsulelayer_kernel(tc, x, w, base, offs, out):
             scale = work.tile([P, H, PIECE], F32, name="scale")
             piece_offsets = offsets[:, p * LIST_COLUMNS : (p + 1) * LIST_COLUMNS]
             for h in range(H):
-                nc.scalar.activation(scale[:, h, :], scale2_psum[h][:], ACT.Sqrt)
+                nc.scalar.activation(scale[:, h, :], inverse2_psum[h][:], ACT.Abs_reciprocal_sqrt)
                 nc.vector.tensor_tensor(
                     windows[h][:].indirect(piece_offsets), s_sbuf[:, h, :], scale[:, h, :], MULT
                 )

@@ -91,7 +91,10 @@ def tile_capsulelayer_kernel(tc, x, w, base, offs, out):
             for h in range(H):
                 nc.tensor.matmul(s_psum[:, h, :], w_scaled[:, h * P : (h + 1) * P], x_sum[:, samples])
             s_sbuf = work.tile([P, H, PIECE], F32, name="s_sbuf")
-            nc.scalar.copy(s_sbuf[:], s_psum[:])
+            if p < PIECES - 1:
+                nc.scalar.copy(s_sbuf[:], s_psum[:])
+            else:
+                nc.vector.tensor_copy(s_sbuf[:], s_psum[:])
             scale = work.tile([P, H, PIECE], F32, name="scale")
             piece_offsets = offsets[:, p * LIST_COLUMNS : (p + 1) * LIST_COLUMNS]
             for h in range(H):

@@ -1,13 +1,14 @@
 import concourse.mybir as mybir
-from concourse.masks import make_identity
 
 F32 = mybir.dt.float32
 BF16 = mybir.dt.bfloat16
 U16 = mybir.dt.uint16
 MULT = mybir.AluOpType.mult
 ADD = mybir.AluOpType.add
+IS_EQUAL = mybir.AluOpType.is_equal
 ACT = mybir.ActivationFunctionType
 
+BLOCK = 32
 P = 128
 N = 256
 R = 16
@@ -48,10 +49,19 @@ def tile_capsulelayer_kernel(tc, x, w, base, offs, out):
             nc.sync.dma_start(window[:], base[h * P : (h + 1) * P, :])
             windows.append(window)
 
+        ones = held.tile([P, BLOCK], F32, name="ones")
+        nc.vector.memset(ones[:], 1.0)
+        count = held.tile([P, BLOCK], F32, name="count", align_bytes=64)
+        nc.vector.tensor_tensor_scan(count[:], ones[:], ones[:], 0.0, MULT, ADD)
+        count_t = held.tile([P, BLOCK], F32, name="count_t", align_bytes=64)
+        nc.vector.transpose(count_t[:], count[:])
         identity = held.tile([P, P], F32, name="identity")
-        make_identity(nc, identity[:])
+        nc.vector.memset(identity[:], 0.0)
+        for b in range(0, P, BLOCK):
+            block = slice(b, b + BLOCK)
+            nc.vector.tensor_tensor(identity[block, block], count_t[block, :], count[block, :], IS_EQUAL)
         warm = held.tile([P, 1], F32, name="warm")
-        nc.gpsimd.memset(warm[:], 1.0)
+        nc.vector.memset(warm[:], 1.0)
         nc.scalar.activation(warm[:], warm[:], ACT.Abs_reciprocal_sqrt)
         w_scaled = held.tile([P, H * P], BF16, name="w_scaled")
         nc.scalar.mul(w_scaled[:], w_raw[:], 1.0 / R)

@@ -76,42 +76,28 @@ def tile_capsulelayer_kernel(tc, x, w, base, offs, out):
 
         for p in range(PIECES):
             samples = slice(p * PIECE, (p + 1) * PIECE)
-            sq = work.tile([P, H], F32, name="sq")
-            for h in range(H):
-                s_by_sample = psum.tile([P, P], F32, name=f"s_by_sample{h}")
-                nc.tensor.matmul(s_by_sample[:], x_sum[:, samples], w_scaled[:, h * P : (h + 1) * P])
-                squares = work.tile([P, P], BF16, name="squares")
-                nc.scalar.activation(squares[:], s_by_sample[:], ACT.Square, accum_out=sq[:, h : h + 1])
-            rsqrt_sq = work.tile([P, H], F32, name="rsqrt_sq")
-            nc.scalar.activation(rsqrt_sq[:], sq[:], ACT.Abs_reciprocal_sqrt)
-            inverse2 = work.tile([P, H], F32, name="inverse2")
-            inverse2_psum = []
-            for h in range(H):
-                column = slice(h, h + 1)
-                nc.scalar.activation(
-                    inverse2[:, column], sq[:, column], ACT.Square,
-                    bias=rsqrt_sq[:, column], scale=rsqrt_sq[:, column],
-                )
-                inverse2_psum.append(psum_factor.tile([P, PIECE], F32, name=f"inverse2_psum{h}"))
-                nc.tensor.transpose(
-                    inverse2_psum[h][:], inverse2[:, column].to_broadcast([P, P]), identity[:]
-                )
-
-            s_psum = psum.tile([P, H, PIECE], F32, name="s_psum")
-            for h in range(H):
-                nc.tensor.matmul(s_psum[:, h, :], w_scaled[:, h * P : (h + 1) * P], x_sum[:, samples])
-            s_sbuf = work.tile([P, H, PIECE], F32, name="s_sbuf")
-            if p < PIECES - 1:
-                nc.scalar.copy(s_sbuf[:], s_psum[:])
-            else:
-                nc.vector.tensor_copy(s_sbuf[:], s_psum[:])
-            scale = work.tile([P, H, PIECE], F32, name="scale")
             piece_offsets = offsets[:, p * LIST_COLUMNS : (p + 1) * LIST_COLUMNS]
             for h in range(H):
-                nc.scalar.activation(scale[:, h, :], inverse2_psum[h][:], ACT.Abs_reciprocal_sqrt)
-                nc.vector.tensor_tensor(
-                    windows[h][:].indirect(piece_offsets), s_sbuf[:, h, :], scale[:, h, :], MULT
-                )
+                w_capsule = w_scaled[:, h * P : (h + 1) * P]
+                s_by_sample = psum.tile([P, P], F32, name="s_by_sample", tag=f"s{h}")
+                nc.tensor.matmul(s_by_sample[:], x_sum[:, samples], w_capsule)
+                squares = work.tile([P, P], BF16, name=f"squares{h}")
+                sq = work.tile([P, 1], F32, name=f"sq{h}")
+                nc.scalar.activation(squares[:], s_by_sample[:], ACT.Square, accum_out=sq[:])
+                rsqrt_sq = work.tile([P, 1], F32, name=f"rsqrt_sq{h}")
+                nc.scalar.activation(rsqrt_sq[:], sq[:], ACT.Abs_reciprocal_sqrt)
+                inverse2 = work.tile([P, 1], F32, name=f"inverse2{h}")
+                nc.scalar.activation(inverse2[:], sq[:], ACT.Square, bias=rsqrt_sq[:], scale=rsqrt_sq[:])
+                inverse2_psum = psum_factor.tile([P, PIECE], F32, name=f"inverse2_psum{h}")
+                nc.tensor.transpose(inverse2_psum[:], inverse2[:].to_broadcast([P, P]), identity[:])
+
+                s_psum = psum.tile([P, PIECE], F32, name="s_psum", tag=f"s{h}")
+                nc.tensor.matmul(s_psum[:], w_capsule, x_sum[:, samples])
+                s_sbuf = work.tile([P, PIECE], F32, name=f"s_sbuf{h}")
+                nc.scalar.copy(s_sbuf[:], s_psum[:])
+                scale = work.tile([P, PIECE], F32, name=f"scale{h}")
+                nc.scalar.activation(scale[:], inverse2_psum[:], ACT.Abs_reciprocal_sqrt)
+                nc.vector.tensor_tensor(windows[h][:].indirect(piece_offsets), s_sbuf[:], scale[:], MULT)
 
         for h in range(H):
             nc.sync.dma_start(out[h * P : (h + 1) * P, :], windows[h][:])

@@ -14,11 +14,12 @@ N = 256
 R = 16
 H = 2
 S = 512
-PIECE = P
-PIECES = N // PIECE
-LIST_COLUMNS = PIECE // 16
+PIECES = (P, P // 2, P // 2)
+assert sum(PIECES) == N
+LIST_ENTRIES = 16
 
-CHUNKS = (32, 32, 32, 32, 32, 32, 32, 16, 16)
+CHUNK = 32
+CHUNKS = (CHUNK,) * (N // CHUNK)
 assert sum(CHUNKS) == N
 
 FLOPS = 2 * P * (H * P) * N
@@ -29,20 +30,21 @@ def tile_capsulelayer_kernel(tc, x, w, base, offs, out):
     with (
         tc.tile_pool(name="held", bufs=1) as held,
         tc.tile_pool(name="xin", bufs=len(CHUNKS)) as xin,
-        tc.tile_pool(name="work", bufs=PIECES) as work,
+        tc.tile_pool(name="work", bufs=len(PIECES)) as work,
         tc.psum_pool(name="psum", bufs=1) as psum,
-        tc.psum_pool(name="psum_factor", bufs=PIECES) as psum_factor,
+        tc.psum_pool(name="psum_factor", bufs=2) as psum_factor,
     ):
         w_raw = held.tile([P, H * P], BF16, name="w_raw")
         nc.scalar.dma_start(w_raw[:], w)
+        offsets = held.tile([P, N // 16], U16, name="offsets")
         x_chunks = []
         for k, size in enumerate(CHUNKS):
             start = sum(CHUNKS[:k])
             x_chunk = xin.tile([P, max(CHUNKS), R], F32, name="x_chunk")
             nc.sync.dma_start(x_chunk[:, :size, :], x[:, start : start + size, :])
             x_chunks.append(x_chunk)
-        offsets = held.tile([P, N // 16], U16, name="offsets")
-        nc.sync.dma_start(offsets[:], offs)
+            if k == 0:
+                nc.sync.dma_start(offsets[:], offs)
         windows = []
         for h in range(H):
             window = held.tile([P, S], F32, name=f"window{h}")
@@ -74,13 +76,16 @@ def tile_capsulelayer_kernel(tc, x, w, base, offs, out):
                     x_sum[:, start : start + size], x_chunks[k][:, :size, :], mybir.AxisListType.X, ADD
                 )
 
-        for p in range(PIECES):
-            samples = slice(p * PIECE, (p + 1) * PIECE)
-            piece_offsets = offsets[:, p * LIST_COLUMNS : (p + 1) * LIST_COLUMNS]
+        for p, size in enumerate(PIECES):
+            start = sum(PIECES[:p])
+            samples = slice(start, start + size)
+            block_samples = slice(start + size - P, start + size)
+            own = slice(P - size, P)
+            piece_offsets = offsets[:, start // LIST_ENTRIES : (start + size) // LIST_ENTRIES]
             for h in range(H):
                 w_capsule = w_scaled[:, h * P : (h + 1) * P]
-                s_by_sample = psum.tile([P, P], F32, name="s_by_sample", tag=f"s{h}")
-                nc.tensor.matmul(s_by_sample[:], x_sum[:, samples], w_capsule)
+                s_by_sample = psum.tile([P, P], F32, name=f"s_by_sample{h}")
+                nc.tensor.matmul(s_by_sample[:], x_sum[:, block_samples], w_capsule)
                 squares = work.tile([P, P], BF16, name=f"squares{h}")
                 sq = work.tile([P, 1], F32, name=f"sq{h}")
                 nc.scalar.activation(squares[:], s_by_sample[:], ACT.Square, accum_out=sq[:])
@@ -88,16 +93,16 @@ def tile_capsulelayer_kernel(tc, x, w, base, offs, out):
                 nc.scalar.activation(rsqrt_sq[:], sq[:], ACT.Abs_reciprocal_sqrt)
                 inverse2 = work.tile([P, 1], F32, name=f"inverse2{h}")
                 nc.scalar.activation(inverse2[:], sq[:], ACT.Square, bias=rsqrt_sq[:], scale=rsqrt_sq[:])
-                inverse2_psum = psum_factor.tile([P, PIECE], F32, name=f"inverse2_psum{h}")
+                inverse2_psum = psum_factor.tile([P, P], F32, name=f"inverse2_psum{h}")
                 nc.tensor.transpose(inverse2_psum[:], inverse2[:].to_broadcast([P, P]), identity[:])
 
-                s_psum = psum.tile([P, PIECE], F32, name="s_psum", tag=f"s{h}")
-                nc.tensor.matmul(s_psum[:], w_capsule, x_sum[:, samples])
-                s_sbuf = work.tile([P, PIECE], F32, name=f"s_sbuf{h}")
-                nc.scalar.copy(s_sbuf[:], s_psum[:])
-                scale = work.tile([P, PIECE], F32, name=f"scale{h}")
-                nc.scalar.activation(scale[:], inverse2_psum[:], ACT.Abs_reciprocal_sqrt)
-                nc.vector.tensor_tensor(windows[h][:].indirect(piece_offsets), s_sbuf[:], scale[:], MULT)
+                s_psum = psum.tile([P, P], F32, name=f"s_psum{h}")
+                nc.tensor.matmul(s_psum[:, :size], w_capsule, x_sum[:, samples])
+                s_sbuf = work.tile([P, P], F32, name=f"s_sbuf{h}")
+                nc.scalar.copy(s_sbuf[:, :size], s_psum[:, :size])
+                scale = work.tile([P, P], F32, name=f"scale{h}")
+                nc.scalar.activation(scale[:, :size], inverse2_psum[:, own], ACT.Abs_reciprocal_sqrt)
+                nc.vector.tensor_tensor(windows[h][:].indirect(piece_offsets), s_sbuf[:, :size], scale[:, :size], MULT)
 
         for h in range(H):
             nc.sync.dma_start(out[h * P : (h + 1) * P, :], windows[h][:])

@@ -35,7 +35,6 @@ def tile_capsulelayer_kernel(tc, x, w, base, offs, out):
         tc.psum_pool(name="psum_factor", bufs=2) as psum_factor,
     ):
         w_raw = held.tile([P, H * P], BF16, name="w_raw")
-        nc.scalar.dma_start(w_raw[:], w)
         offsets = held.tile([P, N // 16], U16, name="offsets")
         x_chunks = []
         for k, size in enumerate(CHUNKS):
@@ -44,6 +43,7 @@ def tile_capsulelayer_kernel(tc, x, w, base, offs, out):
             nc.sync.dma_start(x_chunk[:, :size, :], x[:, start : start + size, :])
             x_chunks.append(x_chunk)
             if k == 0:
+                nc.sync.dma_start(w_raw[:], w)
                 nc.sync.dma_start(offsets[:], offs)
         windows = []
         for h in range(H):

@@ -34,7 +34,7 @@ def tile_capsulelayer_kernel(tc, x, w, base, offs, out):
         tc.psum_pool(name="psum", bufs=1) as psum,
         tc.psum_pool(name="psum_factor", bufs=2) as psum_factor,
     ):
-        w_raw = held.tile([P, H * P], BF16, name="w_raw")
+        w_tile = held.tile([P, H * P], BF16, name="w_tile")
         offsets = held.tile([P, N // 16], U16, name="offsets")
         x_chunks = []
         for k, size in enumerate(CHUNKS):
@@ -43,7 +43,7 @@ def tile_capsulelayer_kernel(tc, x, w, base, offs, out):
             nc.sync.dma_start(x_chunk[:, :size, :], x[:, start : start + size, :])
             x_chunks.append(x_chunk)
             if k == 0:
-                nc.sync.dma_start(w_raw[:], w)
+                nc.sync.dma_start(w_tile[:], w)
                 nc.sync.dma_start(offsets[:], offs)
         windows = []
         for h in range(H):
@@ -65,8 +65,6 @@ def tile_capsulelayer_kernel(tc, x, w, base, offs, out):
         warm = held.tile([P, 1], F32, name="warm")
         nc.vector.memset(warm[:], 1.0)
         nc.scalar.activation(warm[:], warm[:], ACT.Abs_reciprocal_sqrt)
-        w_scaled = held.tile([P, H * P], BF16, name="w_scaled")
-        nc.scalar.mul(w_scaled[:], w_raw[:], 1.0 / R)
 
         x_sum = held.tile([P, N], BF16, name="x_sum")
         with nc.allow_low_precision(reason="the statement rounds xbar to bfloat16"):
@@ -83,12 +81,12 @@ def tile_capsulelayer_kernel(tc, x, w, base, offs, out):
             own = slice(P - size, P)
             piece_offsets = offsets[:, start // LIST_ENTRIES : (start + size) // LIST_ENTRIES]
             for h in range(H):
-                w_capsule = w_scaled[:, h * P : (h + 1) * P]
+                w_capsule = w_tile[:, h * P : (h + 1) * P]
                 s_by_sample = psum.tile([P, P], F32, name=f"s_by_sample{h}")
                 nc.tensor.matmul(s_by_sample[:], x_sum[:, block_samples], w_capsule)
                 squares = work.tile([P, P], BF16, name=f"squares{h}")
                 sq = work.tile([P, 1], F32, name=f"sq{h}")
-                nc.scalar.activation(squares[:], s_by_sample[:], ACT.Square, accum_out=sq[:])
+                nc.scalar.activation(squares[:], s_by_sample[:], ACT.Square, scale=1.0 / R, accum_out=sq[:])
                 rsqrt_sq = work.tile([P, 1], F32, name=f"rsqrt_sq{h}")
                 nc.scalar.activation(rsqrt_sq[:], sq[:], ACT.Abs_reciprocal_sqrt)
                 inverse2 = work.tile([P, 1], F32, name=f"inverse2{h}")
@@ -99,7 +97,7 @@ def tile_capsulelayer_kernel(tc, x, w, base, offs, out):
                 s_psum = psum.tile([P, P], F32, name=f"s_psum{h}")
                 nc.tensor.matmul(s_psum[:, :size], w_capsule, x_sum[:, samples])
                 s_sbuf = work.tile([P, P], F32, name=f"s_sbuf{h}")
-                nc.scalar.copy(s_sbuf[:, :size], s_psum[:, :size])
+                nc.scalar.mul(s_sbuf[:, :size], s_psum[:, :size], 1.0 / R)
                 scale = work.tile([P, P], F32, name=f"scale{h}")
                 nc.scalar.activation(scale[:, :size], inverse2_psum[:, own], ACT.Abs_reciprocal_sqrt)
                 nc.vector.tensor_tensor(windows[h][:].indirect(piece_offsets), s_sbuf[:, :size], scale[:, :size], MULT)

import concourse.mybir as mybir

F32 = mybir.dt.float32
BF16 = mybir.dt.bfloat16
U16 = mybir.dt.uint16
MULT = mybir.AluOpType.mult
ADD = mybir.AluOpType.add
IS_EQUAL = mybir.AluOpType.is_equal
ACT = mybir.ActivationFunctionType

BLOCK = 32
P = 128
N = 256
R = 16
H = 2
S = 512
PIECES = (P, P // 2, P // 2)
assert sum(PIECES) == N
LIST_ENTRIES = 16

CHUNK = 32
CHUNKS = (CHUNK,) * (N // CHUNK)
assert sum(CHUNKS) == N

FLOPS = 2 * P * (H * P) * N


def tile_capsulelayer_kernel(tc, x, w, base, offs, out):
    nc = tc.nc
    with (
        tc.tile_pool(name="held", bufs=1) as held,
        tc.tile_pool(name="xin", bufs=len(CHUNKS)) as xin,
        tc.tile_pool(name="work", bufs=len(PIECES)) as work,
        tc.psum_pool(name="psum", bufs=1) as psum,
        tc.psum_pool(name="psum_factor", bufs=2) as psum_factor,
    ):
        w_tile = held.tile([P, H * P], BF16, name="w_tile")
        offsets = held.tile([P, N // 16], U16, name="offsets")
        x_chunks = []
        for k, size in enumerate(CHUNKS):
            start = sum(CHUNKS[:k])
            x_chunk = xin.tile([P, max(CHUNKS), R], F32, name="x_chunk")
            nc.sync.dma_start(x_chunk[:, :size, :], x[:, start : start + size, :])
            x_chunks.append(x_chunk)
            if k == 0:
                nc.sync.dma_start(w_tile[:], w)
                nc.sync.dma_start(offsets[:], offs)
        windows = []
        for h in range(H):
            window = held.tile([P, S], F32, name=f"window{h}")
            nc.sync.dma_start(window[:], base[h * P : (h + 1) * P, :])
            windows.append(window)

        ones = held.tile([P, BLOCK], F32, name="ones")
        nc.vector.memset(ones[:], 1.0)
        count = held.tile([P, BLOCK], F32, name="count", align_bytes=64)
        nc.vector.tensor_tensor_scan(count[:], ones[:], ones[:], 0.0, MULT, ADD)
        count_t = held.tile([P, BLOCK], F32, name="count_t", align_bytes=64)
        nc.vector.transpose(count_t[:], count[:])
        identity = held.tile([P, P], F32, name="identity")
        nc.vector.memset(identity[:], 0.0)
        for b in range(0, P, BLOCK):
            block = slice(b, b + BLOCK)
            nc.vector.tensor_tensor(identity[block, block], count_t[block, :], count[block, :], IS_EQUAL)
        warm = held.tile([P, 1], F32, name="warm")
        nc.vector.memset(warm[:], 1.0)
        nc.scalar.activation(warm[:], warm[:], ACT.Abs_reciprocal_sqrt)

        x_sum = held.tile([P, N], BF16, name="x_sum")
        with nc.allow_low_precision(reason="the statement rounds xbar to bfloat16"):
            for k, size in enumerate(CHUNKS):
                start = sum(CHUNKS[:k])
                nc.vector.tensor_reduce(
                    x_sum[:, start : start + size], x_chunks[k][:, :size, :], mybir.AxisListType.X, ADD
                )

        for p, size in enumerate(PIECES):
            start = sum(PIECES[:p])
            samples = slice(start, start + size)
            block_samples = slice(start + size - P, start + size)
            own = slice(P - size, P)
            piece_offsets = offsets[:, start // LIST_ENTRIES : (start + size) // LIST_ENTRIES]
            for h in range(H):
                w_capsule = w_tile[:, h * P : (h + 1) * P]
                s_by_sample = psum.tile([P, P], F32, name=f"s_by_sample{h}")
                nc.tensor.matmul(s_by_sample[:], x_sum[:, block_samples], w_capsule)
                squares = work.tile([P, P], BF16, name=f"squares{h}")
                sq = work.tile([P, 1], F32, name=f"sq{h}")
                nc.scalar.activation(squares[:], s_by_sample[:], ACT.Square, scale=1.0 / R, accum_out=sq[:])
                rsqrt_sq = work.tile([P, 1], F32, name=f"rsqrt_sq{h}")
                nc.scalar.activation(rsqrt_sq[:], sq[:], ACT.Abs_reciprocal_sqrt)
                inverse2 = work.tile([P, 1], F32, name=f"inverse2{h}")
                nc.scalar.activation(inverse2[:], sq[:], ACT.Square, bias=rsqrt_sq[:], scale=rsqrt_sq[:])
                inverse2_psum = psum_factor.tile([P, P], F32, name=f"inverse2_psum{h}")
                nc.tensor.transpose(inverse2_psum[:], inverse2[:].to_broadcast([P, P]), identity[:])

                s_psum = psum.tile([P, P], F32, name=f"s_psum{h}")
                nc.tensor.matmul(s_psum[:, :size], w_capsule, x_sum[:, samples])
                s_sbuf = work.tile([P, P], F32, name=f"s_sbuf{h}")
                nc.scalar.mul(s_sbuf[:, :size], s_psum[:, :size], 1.0 / R)
                scale = work.tile([P, P], F32, name=f"scale{h}")
                nc.scalar.activation(scale[:, :size], inverse2_psum[:, own], ACT.Abs_reciprocal_sqrt)
                nc.vector.tensor_tensor(windows[h][:].indirect(piece_offsets), s_sbuf[:, :size], scale[:, :size], MULT)

        for h in range(H):
            nc.sync.dma_start(out[h * P : (h + 1) * P, :], windows[h][:])
